import numpy as np
import ml_dtypes


def mxq(x, axis, fmt="e4m3"):
    dtype, down = {"e4m3": (ml_dtypes.float8_e4m3fn, 7), "e5m2": (ml_dtypes.float8_e5m2, 14)}[fmt]
    v = np.moveaxis(np.asarray(x, np.float32).astype(ml_dtypes.bfloat16).astype(np.float64), axis, -1)
    blocks = v.reshape(v.shape[:-1] + (-1, 32))
    amax = np.abs(blocks).max(-1, keepdims=True)
    byte = np.maximum(np.where(amax > 0, np.frexp(amax)[1] - 1 + 127, 0) - down, 1)
    scale = np.exp2(byte - 127.0)
    codes = (blocks / scale).astype(np.float32).astype(dtype).astype(np.float64)
    return np.moveaxis((codes * scale).reshape(v.shape), -1, axis)


WIDE = False


def mx_kscale(k):
    if not WIDE:
        return np.ones(k)
    levels = np.array([10, -10, 5, -5, 0])
    a = np.random.permutation(np.resize(levels, k // 512 * 4)).reshape(k // 512, 4)
    idx = np.arange(k)
    return np.exp2(a[idx // 512, idx % 128 // 32])


BF16 = ml_dtypes.bfloat16


def bf(x):
    return np.asarray(x, np.float32).astype(BF16)


def f64(x):
    return np.asarray(x).astype(np.float64)


B, T, D, H = 4, 256, 512, 2048
N = B * T
EMA0 = 1.0


def sigmoid(v):
    return 1.0 / (1.0 + np.exp(-v))


def surprise_gate(err):
    err_mag = np.sqrt(np.sum(err * err)) / N
    ema = 0.95 * EMA0 + 0.05 * err_mag
    return np.minimum(err_mag / np.maximum(ema, 1e-8), 3.0)


def setup_inputs():
    s, t = mx_kscale(D), mx_kscale(N)
    return {"err": bf(np.random.standard_normal((N, D)) * 2.3 * s[None, :] * t[:, None]),
            "W_down": bf(np.random.standard_normal((D, H)) / np.sqrt(D) / s[:, None]),
            "gate_pre": bf(np.random.standard_normal((N, H))),
            "up_pre": bf(np.random.standard_normal((N, H))),
            "x_pred": bf(np.random.standard_normal((N, D)) / t[:, None])}


def reference(err, W_down, gate_pre, up_pre, x_pred):
    err, gate_pre, up_pre = f64(err), f64(gate_pre), f64(up_pre)
    sg = surprise_gate(err)
    d_h = mxq(err, 1, "e4m3") @ mxq(f64(W_down), 0, "e4m3")
    sig = sigmoid(gate_pre)
    gate_act = gate_pre * sig
    d_gate_act = d_h * up_pre
    d_up_val = d_h * gate_act
    d_gate_pre = d_gate_act * sig * (1.0 + gate_pre * (1.0 - sig))
    xq = mxq(f64(x_pred), 0, "e4m3")
    grad_gate = (mxq(d_gate_pre, 0, "e4m3").T @ xq) / N
    grad_up = (mxq(d_up_val, 0, "e4m3").T @ xq) / N
    return grad_up * sg, grad_gate * sg

@@ -1,0 +1,232 @@
+from contextlib import ExitStack
+
+import concourse.mybir as mybir
+from concourse.masks import make_identity
+
+FP32 = mybir.dt.float32
+BF16 = mybir.dt.bfloat16
+U32 = mybir.dt.uint32
+U8 = mybir.dt.uint8
+FP8X4 = mybir.dt.float8_e4m3fn_x4
+ACT = mybir.ActivationFunctionType
+ALU = mybir.AluOpType
+
+P = 128
+PACK = 4
+K_PASS = P * PACK
+TOKENS, FEATURES, HIDDEN = 1024, 512, 2048
+TOKEN_PASSES = TOKENS // K_PASS
+H_CHUNK = 512
+H_CHUNKS = HIDDEN // H_CHUNK
+M_TILES = H_CHUNK // P
+UNIT = PACK * H_CHUNK
+RUN = 4
+
+FLOPS = 3 * 2 * TOKENS * FEATURES * HIDDEN
+
+
+def by_column(rows):
+    return rows.rearrange("p t (c i) -> p c t i", i=RUN)
+
+
+def by_word(grouped):
+    return grouped.rearrange("p (c i t) -> p c t i", i=RUN, t=PACK)
+
+
+def tile_continuummemorysystem_pa_kernel(tc, err, W_down, gate_pre, up_pre, x_pred, out_0, out_1):
+    nc = tc.nc
+    with ExitStack() as pools:
+        const = pools.enter_context(tc.tile_pool(name="const", bufs=1))
+        inputs = pools.enter_context(tc.tile_pool(name="inputs", bufs=1))
+        codes = pools.enter_context(tc.tile_pool(name="codes", bufs=1))
+        chunk_codes = pools.enter_context(tc.tile_pool(name="chunk_codes", bufs=2))
+        grouped_pool = pools.enter_context(tc.tile_pool(name="grouped", bufs=6))
+        work = pools.enter_context(tc.tile_pool(name="work", bufs=3))
+        results = pools.enter_context(tc.tile_pool(name="results", bufs=6))
+        psum_first = pools.enter_context(tc.psum_pool(name="psum_first", bufs=4))
+        psum_second = pools.enter_context(tc.psum_pool(name="psum_second", bufs=4))
+
+        err_sb, x_sb, w_sb, gate_sb, up_sb = {}, {}, {}, {}, {}
+
+        def load_err(c):
+            err_sb[c] = inputs.tile([P, PACK * FEATURES], BF16, name="err_%d" % c)
+            rows = err[c * K_PASS : (c + 1) * K_PASS, :]
+            nc.sync.dma_start(out=err_sb[c][:], in_=rows.rearrange("(p j) d -> p (j d)", j=PACK))
+
+        def load_x(c):
+            x_sb[c] = inputs.tile([P, PACK, FEATURES], BF16, name="x_%d" % c)
+            rows = x_pred[c * K_PASS : (c + 1) * K_PASS, :]
+            nc.sync.dma_start(out=x_sb[c][:], in_=rows.rearrange("(p j) d -> p j d", j=PACK))
+
+        def load_w(hc):
+            w_sb[hc] = inputs.tile([P, PACK, H_CHUNK], BF16, name="w_%d" % hc)
+            cols = slice(hc * H_CHUNK, (hc + 1) * H_CHUNK)
+            for u in range(2):
+                rows = W_down[u * 2 * P : (u + 1) * 2 * P, cols]
+                nc.sync.dma_start(out=w_sb[hc][:, 2 * u : 2 * u + 2, :], in_=rows.rearrange("(q e) n -> q e n", e=2))
+
+        def load_pre(hc, c):
+            cols = slice(hc * H_CHUNK, (hc + 1) * H_CHUNK)
+            toks = slice(c * K_PASS, (c + 1) * K_PASS)
+            gate_sb[hc, c] = inputs.tile([P, PACK, H_CHUNK], BF16, name="gate_%d_%d" % (hc, c))
+            nc.sync.dma_start(out=gate_sb[hc, c][:], in_=gate_pre[toks, cols].rearrange("(p j) h -> p j h", j=PACK))
+            up_sb[hc, c] = inputs.tile([P, PACK, H_CHUNK], BF16, name="up_%d_%d" % (hc, c))
+            nc.sync.dma_start(out=up_sb[hc, c][:], in_=up_pre[toks, cols].rearrange("(p j) h -> p j h", j=PACK))
+
+        load_err(0)
+        load_w(0)
+        load_pre(0, 0)
+        load_err(1)
+        load_pre(0, 1)
+        load_x(0)
+        load_x(1)
+        for hc in range(1, H_CHUNKS):
+            load_w(hc)
+            load_pre(hc, 0)
+            load_pre(hc, 1)
+
+        identity = const.tile([P, P], FP32)
+        make_identity(nc, identity[:])
+
+        err_codes = codes.tile([P, TOKEN_PASSES, K_PASS], U32, align_bytes=64)
+        err_scales = codes.tile([P, TOKEN_PASSES, K_PASS], U8, align_bytes=64)
+        x_codes = codes.tile([P, TOKEN_PASSES, FEATURES], U32, align_bytes=64)
+        x_scales = codes.tile([P, TOKEN_PASSES, FEATURES], U8, align_bytes=64)
+        w_codes = codes.tile([P, H_CHUNKS, H_CHUNK], U32, align_bytes=64)
+        w_scales = codes.tile([P, H_CHUNKS, H_CHUNK], U8, align_bytes=64)
+
+        def quantise(grouped, words, scales):
+            nc.vector.quantize_mx(out=words.bitcast(FP8X4), scales=scales, in_=grouped[:])
+
+        def prepare_err(c):
+            err_words = err_sb[c][:].bitcast(FP32)
+            grouped = grouped_pool.tile([P, UNIT], BF16, tag="grouped", align_bytes=64)
+            grouped_words = grouped[:].bitcast(FP32).rearrange("q (j p u) -> q j p u", j=PACK, u=2)
+            for pair in range(PACK // 2):
+                turned = psum_first.tile([P, 2, 2, P], FP32, tag="first")
+                for b in range(2):
+                    j = 2 * pair + b
+                    for u in range(2):
+                        first_word = (2 * j + u) * P
+                        nc.tensor.transpose(turned[:, b, u, :], err_words[:, first_word : first_word + P], identity[:])
+                nc.scalar.copy(
+                    out=grouped_words[:, 2 * pair : 2 * pair + 2, :, :],
+                    in_=turned[:].rearrange("q b u p -> q b p u"),
+                )
+            quantise(grouped, err_codes[:, c, :], err_scales[:, c, :])
+
+        def prepare_rows(copy, rows, words, scales):
+            grouped = grouped_pool.tile([P, UNIT], BF16, tag="grouped", align_bytes=64)
+            copy(out=by_word(grouped[:]), in_=by_column(rows[:]))
+            quantise(grouped, words, scales)
+
+        final_scale = const.tile([P, 2], FP32)
+
+        def surprise_gate():
+            square_sums = const.tile([P, TOKEN_PASSES], FP32)
+            for c in range(TOKEN_PASSES):
+                squares = work.tile([P, UNIT], FP32, tag="silu")
+                nc.scalar.activation(out=squares[:], in_=err_sb[c][:], func=ACT.Square, accum_out=square_sums[:, c : c + 1])
+            row_sum = const.tile([P, 1], FP32)
+            nc.vector.reduce_sum(out=row_sum[:], in_=square_sums[:], axis=mybir.AxisListType.X)
+            repeated = const.tile([P, P], FP32)
+            nc.vector.tensor_copy(out=repeated[:], in_=row_sum[:, 0:1].to_broadcast([P, P]))
+            turned = psum_second.tile([P, P], FP32, tag="second")
+            nc.tensor.transpose(turned[:], repeated[:], identity[:])
+            total = const.tile([P, 1], FP32)
+            nc.vector.reduce_sum(out=total[:], in_=turned[:], axis=mybir.AxisListType.X)
+            err_mag = const.tile([P, 1], FP32)
+            nc.scalar.activation(out=err_mag[:], in_=total[:], func=ACT.Sqrt, scale=1.0 / (TOKENS * TOKENS))
+            ema = const.tile([P, 1], FP32)
+            nc.vector.tensor_scalar(out=ema[:], in0=err_mag[:], scalar1=0.05, scalar2=0.95, op0=ALU.mult, op1=ALU.add)
+            nc.vector.tensor_scalar_max(out=ema[:], in0=ema[:], scalar1=1e-8)
+            inverse = const.tile([P, 1], FP32)
+            nc.vector.reciprocal(out=inverse[:], in_=ema[:])
+            ratio = const.tile([P, 1], FP32)
+            nc.vector.tensor_mul(out=ratio[:], in0=err_mag[:], in1=inverse[:])
+            for column, factor in ((0, 2.0), (1, -2.0)):
+                nc.vector.tensor_scalar(
+                    out=final_scale[:, column : column + 1], in0=ratio[:],
+                    scalar1=3.0, scalar2=1.0 / (factor * TOKENS), op0=ALU.min, op1=ALU.mult,
+                )
+
+        tanh_tiles, silu_tiles = {}, {}
+
+        def gate_functions(hc, c):
+            gate_flat = gate_sb[hc, c][:].rearrange("p j h -> p (j h)")
+            tanh_tiles[hc, c] = work.tile([P, UNIT], FP32, tag="tanh", name="tanh_half")
+            nc.scalar.activation(out=tanh_tiles[hc, c][:], in_=gate_flat, func=ACT.Tanh, scale=0.5)
+            silu_tiles[hc, c] = work.tile([P, UNIT], FP32, tag="silu", name="silu_neg")
+            nc.scalar.activation(out=silu_tiles[hc, c][:], in_=gate_flat, func=ACT.Silu, scale=-1.0)
+
+        def pointwise(hc, c, up_words, up_planes, gate_words, gate_planes):
+            gate_factor = silu_tiles[hc, c]
+            nc.vector.scalar_tensor_tensor(
+                out=gate_factor[:], in0=gate_factor[:], scalar=1.0, in1=up_sb[hc, c][:].rearrange("p j h -> p (j h)"),
+                op0=ALU.subtract, op1=ALU.mult,
+            )
+            half = tanh_tiles[hc, c]
+            for j in range(PACK):
+                d_h = psum_first.tile([P, H_CHUNK], FP32, tag="first")
+                nc.tensor.matmul_mx(
+                    out=d_h[:],
+                    lhsT=err_codes[:, c, j * P : (j + 1) * P].bitcast(FP8X4),
+                    lhsT_scale=err_scales[:, c, j * P : (j + 1) * P],
+                    rhs=w_codes[:, hc, :].bitcast(FP8X4),
+                    rhs_scale=w_scales[:, hc, :],
+                    start=True,
+                    stop=True,
+                )
+                cols = slice(j * H_CHUNK, (j + 1) * H_CHUNK)
+                nc.vector.scalar_tensor_tensor(
+                    out=half[:, cols], in0=half[:, cols], scalar=1.0, in1=d_h[:], op0=ALU.add, op1=ALU.mult,
+                )
+            half_rows = half[:].rearrange("p (j h) -> p j h", j=PACK)
+            d_up = grouped_pool.tile([P, UNIT], BF16, tag="grouped", align_bytes=64)
+            nc.vector.tensor_tensor(out=by_word(d_up[:]), in0=by_column(half_rows), in1=by_column(gate_sb[hc, c][:]), op=ALU.mult)
+            d_gate = grouped_pool.tile([P, UNIT], BF16, tag="grouped", align_bytes=64)
+            factor_rows = gate_factor[:].rearrange("p (j h) -> p j h", j=PACK)
+            nc.vector.tensor_tensor(out=by_word(d_gate[:]), in0=by_column(half_rows), in1=by_column(factor_rows), op=ALU.mult)
+            quantise(d_up, up_words[:, c, :], up_planes[:, c, :])
+            quantise(d_gate, gate_words[:, c, :], gate_planes[:, c, :])
+
+        def second_products(hc, words, planes, column, out):
+            for m in range(M_TILES):
+                acc = psum_second.tile([P, FEATURES], FP32, tag="second")
+                for c in range(TOKEN_PASSES):
+                    nc.tensor.matmul_mx(
+                        out=acc[:],
+                        lhsT=words[:, c, m * P : (m + 1) * P].bitcast(FP8X4),
+                        lhsT_scale=planes[:, c, m * P : (m + 1) * P],
+                        rhs=x_codes[:, c, :].bitcast(FP8X4),
+                        rhs_scale=x_scales[:, c, :],
+                        start=(c == 0),
+                        stop=(c == TOKEN_PASSES - 1),
+                    )
+                scaled = results.tile([P, FEATURES], FP32)
+                nc.scalar.activation(out=scaled[:], in_=acc[:], func=ACT.Copy, scale=final_scale[:, column : column + 1])
+                first_row = hc * H_CHUNK + m * P
+                nc.sync.dma_start(out=out[first_row : first_row + P, :], in_=scaled[:])
+
+        prepare_err(0)
+        prepare_rows(nc.vector.tensor_copy, w_sb[0], w_codes[:, 0, :], w_scales[:, 0, :])
+        gate_functions(0, 0)
+        prepare_err(1)
+        gate_functions(0, 1)
+        for hc in range(H_CHUNKS):
+            up_words = chunk_codes.tile([P, TOKEN_PASSES, H_CHUNK], U32, align_bytes=64)
+            up_planes = chunk_codes.tile([P, TOKEN_PASSES, H_CHUNK], U8, align_bytes=64)
+            gate_words = chunk_codes.tile([P, TOKEN_PASSES, H_CHUNK], U32, align_bytes=64)
+            gate_planes = chunk_codes.tile([P, TOKEN_PASSES, H_CHUNK], U8, align_bytes=64)
+            for c in range(TOKEN_PASSES):
+                pointwise(hc, c, up_words, up_planes, gate_words, gate_planes)
+                if hc + 1 < H_CHUNKS:
+                    gate_functions(hc + 1, c)
+                if hc == 0 and c == 0:
+                    surprise_gate()
+                    for cx in range(TOKEN_PASSES):
+                        prepare_rows(nc.scalar.copy, x_sb[cx], x_codes[:, cx, :], x_scales[:, cx, :])
+                if hc + 1 < H_CHUNKS and c == 0:
+                    prepare_rows(nc.scalar.copy, w_sb[hc + 1], w_codes[:, hc + 1, :], w_scales[:, hc + 1, :])
+            second_products(hc, up_words, up_planes, 0, out_0)
+            second_products(hc, gate_words, gate_planes, 1, out_1)

@@ -20,6 +20,8 @@ H_CHUNK = 512
 H_CHUNKS = HIDDEN // H_CHUNK
 M_TILES = H_CHUNK // P
 UNIT = PACK * H_CHUNK
+UNITS = H_CHUNKS * TOKEN_PASSES
+HALF_UNIT = UNIT // 2
 RUN = 4
 
 FLOPS = 3 * 2 * TOKENS * FEATURES * HIDDEN
@@ -35,16 +37,20 @@ def by_word(grouped):
 
 def tile_continuummemorysystem_pa_kernel(tc, err, W_down, gate_pre, up_pre, x_pred, out_0, out_1):
     nc = tc.nc
+    outs = (out_0, out_1)
     with ExitStack() as pools:
         const = pools.enter_context(tc.tile_pool(name="const", bufs=1))
         inputs = pools.enter_context(tc.tile_pool(name="inputs", bufs=1))
         codes = pools.enter_context(tc.tile_pool(name="codes", bufs=1))
         chunk_codes = pools.enter_context(tc.tile_pool(name="chunk_codes", bufs=2))
-        grouped_pool = pools.enter_context(tc.tile_pool(name="grouped", bufs=6))
+        grouped_pool = pools.enter_context(tc.tile_pool(name="grouped", bufs=3))
+        pair_pool = pools.enter_context(tc.tile_pool(name="pair", bufs=1))
         work = pools.enter_context(tc.tile_pool(name="work", bufs=3))
         results = pools.enter_context(tc.tile_pool(name="results", bufs=6))
         psum_first = pools.enter_context(tc.psum_pool(name="psum_first", bufs=4))
-        psum_second = pools.enter_context(tc.psum_pool(name="psum_second", bufs=4))
+        psum_up = pools.enter_context(tc.psum_pool(name="psum_up", bufs=2))
+        psum_second = pools.enter_context(tc.psum_pool(name="psum_second", bufs=2))
+        pools.enter_context(tc.manual_schedule())
 
         err_sb, x_sb, w_sb, gate_sb, up_sb = {}, {}, {}, {}, {}
 
@@ -65,28 +71,49 @@ def tile_continuummemorysystem_pa_kernel(tc, err, W_down, gate_pre, up_pre, x_pr
                 rows = W_down[u * 2 * P : (u + 1) * 2 * P, cols]
                 nc.sync.dma_start(out=w_sb[hc][:, 2 * u : 2 * u + 2, :], in_=rows.rearrange("(q e) n -> q e n", e=2))
 
-        def load_pre(hc, c):
+        def load_pre(kept, source, label, u):
+            hc, c = u // TOKEN_PASSES, u % TOKEN_PASSES
             cols = slice(hc * H_CHUNK, (hc + 1) * H_CHUNK)
             toks = slice(c * K_PASS, (c + 1) * K_PASS)
-            gate_sb[hc, c] = inputs.tile([P, PACK, H_CHUNK], BF16, name="gate_%d_%d" % (hc, c))
-            nc.sync.dma_start(out=gate_sb[hc, c][:], in_=gate_pre[toks, cols].rearrange("(p j) h -> p j h", j=PACK))
-            up_sb[hc, c] = inputs.tile([P, PACK, H_CHUNK], BF16, name="up_%d_%d" % (hc, c))
-            nc.sync.dma_start(out=up_sb[hc, c][:], in_=up_pre[toks, cols].rearrange("(p j) h -> p j h", j=PACK))
+            kept[u] = inputs.tile([P, PACK, H_CHUNK], BF16, name="%s_%d" % (label, u))
+            nc.sync.dma_start(out=kept[u][:], in_=source[toks, cols].rearrange("(p j) h -> p j h", j=PACK))
 
+        def load_gate(u):
+            load_pre(gate_sb, gate_pre, "gate", u)
+
+        def load_up(u):
+            load_pre(up_sb, up_pre, "up", u)
+
+        load_gate(0)
         load_err(0)
-        load_w(0)
-        load_pre(0, 0)
         load_err(1)
-        load_pre(0, 1)
+        load_w(0)
+        load_up(0)
+        load_gate(1)
+        load_up(1)
+        load_w(1)
+        load_gate(2)
+        load_up(2)
         load_x(0)
         load_x(1)
-        for hc in range(1, H_CHUNKS):
+        load_gate(3)
+        load_up(3)
+        for hc in range(2, H_CHUNKS):
             load_w(hc)
-            load_pre(hc, 0)
-            load_pre(hc, 1)
+            for u in (2 * hc, 2 * hc + 1):
+                load_gate(u)
+                load_up(u)
 
+        warm = const.tile([P, 1], FP32)
+        nc.gpsimd.memset(warm[:], 0.0)
         identity = const.tile([P, P], FP32)
         make_identity(nc, identity[:])
+        identity_bf = const.tile([P, P], BF16)
+        make_identity(nc, identity_bf[:])
+        one_half = const.tile([P, 1], FP32)
+        nc.gpsimd.memset(one_half[:], 0.5)
+        warmed = const.tile([P, 1], FP32)
+        nc.scalar.activation(out=warmed[:], in_=warm[:], func=ACT.Tanh)
 
         err_codes = codes.tile([P, TOKEN_PASSES, K_PASS], U32, align_bytes=64)
         err_scales = codes.tile([P, TOKEN_PASSES, K_PASS], U8, align_bytes=64)
@@ -96,47 +123,68 @@ def tile_continuummemorysystem_pa_kernel(tc, err, W_down, gate_pre, up_pre, x_pr
         w_scales = codes.tile([P, H_CHUNKS, H_CHUNK], U8, align_bytes=64)
 
         def quantise(grouped, words, scales):
-            nc.vector.quantize_mx(out=words.bitcast(FP8X4), scales=scales, in_=grouped[:])
+            nc.vector.quantize_mx(out=words.bitcast(FP8X4), scales=scales, in_=grouped)
 
-        def prepare_err(c):
+        turned_err, grouped_err, grouped_rows = {}, {}, {}
+
+        def transpose_err(c):
             err_words = err_sb[c][:].bitcast(FP32)
-            grouped = grouped_pool.tile([P, UNIT], BF16, tag="grouped", align_bytes=64)
-            grouped_words = grouped[:].bitcast(FP32).rearrange("q (j p u) -> q j p u", j=PACK, u=2)
+            turned_err[c] = []
             for pair in range(PACK // 2):
-                turned = psum_first.tile([P, 2, 2, P], FP32, tag="first")
+                turned = psum_first.tile([P, 2, 2, P], FP32, tag="first", name="turned")
                 for b in range(2):
                     j = 2 * pair + b
                     for u in range(2):
                         first_word = (2 * j + u) * P
                         nc.tensor.transpose(turned[:, b, u, :], err_words[:, first_word : first_word + P], identity[:])
-                nc.scalar.copy(
-                    out=grouped_words[:, 2 * pair : 2 * pair + 2, :, :],
-                    in_=turned[:].rearrange("q b u p -> q b p u"),
-                )
-            quantise(grouped, err_codes[:, c, :], err_scales[:, c, :])
+                turned_err[c].append(turned)
 
-        def prepare_rows(copy, rows, words, scales):
-            grouped = grouped_pool.tile([P, UNIT], BF16, tag="grouped", align_bytes=64)
-            copy(out=by_word(grouped[:]), in_=by_column(rows[:]))
-            quantise(grouped, words, scales)
+        def regroup_err(c):
+            grouped = grouped_pool.tile([P, UNIT], BF16, tag="grouped", align_bytes=64, name="grouped")
+            grouped_words = grouped[:].bitcast(FP32).rearrange("q (j p u) -> q j p u", j=PACK, u=2)
+            for pair in range(PACK // 2):
+                nc.vector.tensor_copy(
+                    out=grouped_words[:, 2 * pair : 2 * pair + 2, :, :],
+                    in_=turned_err[c][pair][:].rearrange("q b u p -> q b p u"),
+                )
+            grouped_err[c] = grouped
+
+        def regroup_rows(key, rows):
+            grouped = grouped_pool.tile([P, UNIT], BF16, tag="grouped", align_bytes=64, name="grouped")
+            nc.scalar.copy(out=by_word(grouped[:]), in_=by_column(rows[:]))
+            grouped_rows[key] = grouped
 
         final_scale = const.tile([P, 2], FP32)
+        square_bank = psum_second.tile([P, P], FP32, tag="second", name="square_bank")
+        repeated = const.tile([P, P], FP32)
+        scaled_total = const.tile([P, 1], FP32)
+        err_mag = const.tile([P, 1], FP32)
 
-        def surprise_gate():
-            square_sums = const.tile([P, TOKEN_PASSES], FP32)
-            for c in range(TOKEN_PASSES):
-                squares = work.tile([P, UNIT], FP32, tag="silu")
-                nc.scalar.activation(out=squares[:], in_=err_sb[c][:], func=ACT.Square, accum_out=square_sums[:, c : c + 1])
+        def squares(c):
+            for j in range(PACK):
+                for b in range(FEATURES // P):
+                    block = err_sb[c][:, j * FEATURES + b * P : j * FEATURES + (b + 1) * P]
+                    nc.tensor.matmul(
+                        out=square_bank[:], lhsT=block, rhs=block,
+                        start=(c == 0 and j == 0 and b == 0),
+                        stop=(c == TOKEN_PASSES - 1 and j == PACK - 1 and b == FEATURES // P - 1),
+                    )
+
+        def diagonal_sums():
+            masked = const.tile([P, P], FP32)
             row_sum = const.tile([P, 1], FP32)
-            nc.vector.reduce_sum(out=row_sum[:], in_=square_sums[:], axis=mybir.AxisListType.X)
-            repeated = const.tile([P, P], FP32)
+            nc.vector.scalar_tensor_tensor(
+                out=masked[:], in0=square_bank[:], scalar=1.0, in1=identity[:], op0=ALU.mult, op1=ALU.mult,
+                accum_out=row_sum[:],
+            )
             nc.vector.tensor_copy(out=repeated[:], in_=row_sum[:, 0:1].to_broadcast([P, P]))
-            turned = psum_second.tile([P, P], FP32, tag="second")
-            nc.tensor.transpose(turned[:], repeated[:], identity[:])
+
+        def total_of_squares(turned):
             total = const.tile([P, 1], FP32)
             nc.vector.reduce_sum(out=total[:], in_=turned[:], axis=mybir.AxisListType.X)
-            err_mag = const.tile([P, 1], FP32)
-            nc.scalar.activation(out=err_mag[:], in_=total[:], func=ACT.Sqrt, scale=1.0 / (TOKENS * TOKENS))
+            nc.vector.tensor_scalar_mul(out=scaled_total[:], in0=total[:], scalar1=1.0 / (TOKENS * TOKENS))
+
+        def surprise_gate():
             ema = const.tile([P, 1], FP32)
             nc.vector.tensor_scalar(out=ema[:], in0=err_mag[:], scalar1=0.05, scalar2=0.95, op0=ALU.mult, op1=ALU.add)
             nc.vector.tensor_scalar_max(out=ema[:], in0=ema[:], scalar1=1e-8)
@@ -150,24 +198,53 @@ def tile_continuummemorysystem_pa_kernel(tc, err, W_down, gate_pre, up_pre, x_pr
                     scalar1=3.0, scalar2=1.0 / (factor * TOKENS), op0=ALU.min, op1=ALU.mult,
                 )
 
-        tanh_tiles, silu_tiles = {}, {}
+        tanh_tiles, silu_tiles, d_h_banks, up_banks, pair_tiles, chunk_tiles = {}, {}, {}, {}, {}, {}
 
-        def gate_functions(hc, c):
-            gate_flat = gate_sb[hc, c][:].rearrange("p j h -> p (j h)")
-            tanh_tiles[hc, c] = work.tile([P, UNIT], FP32, tag="tanh", name="tanh_half")
-            nc.scalar.activation(out=tanh_tiles[hc, c][:], in_=gate_flat, func=ACT.Tanh, scale=0.5)
-            silu_tiles[hc, c] = work.tile([P, UNIT], FP32, tag="silu", name="silu_neg")
-            nc.scalar.activation(out=silu_tiles[hc, c][:], in_=gate_flat, func=ACT.Silu, scale=-1.0)
+        def silu_piece(u, piece):
+            if piece == 0:
+                silu_tiles[u] = work.tile([P, UNIT], FP32, tag="silu", name="silu_neg")
+            cols = slice(piece * HALF_UNIT, (piece + 1) * HALF_UNIT)
+            gate_flat = gate_sb[u][:].rearrange("p j h -> p (j h)")
+            nc.scalar.activation(out=silu_tiles[u][:, cols], in_=gate_flat[:, cols], func=ACT.Silu, scale=-1.0)
 
-        def pointwise(hc, c, up_words, up_planes, gate_words, gate_planes):
-            gate_factor = silu_tiles[hc, c]
-            nc.vector.scalar_tensor_tensor(
-                out=gate_factor[:], in0=gate_factor[:], scalar=1.0, in1=up_sb[hc, c][:].rearrange("p j h -> p (j h)"),
-                op0=ALU.subtract, op1=ALU.mult,
-            )
-            half = tanh_tiles[hc, c]
+        def tanh_piece(u, piece):
+            if piece == 0:
+                tanh_tiles[u] = work.tile([P, UNIT], FP32, tag="tanh", name="tanh_half")
+            cols = slice(piece * HALF_UNIT, (piece + 1) * HALF_UNIT)
+            gate_flat = gate_sb[u][:].rearrange("p j h -> p (j h)")
+            nc.scalar.activation(out=tanh_tiles[u][:, cols], in_=gate_flat[:, cols], func=ACT.Tanh, scale=0.5)
+
+        def gate_function_pieces(u):
+            return [(silu_piece, u, 0), (silu_piece, u, 1), (tanh_piece, u, 0), (tanh_piece, u, 1)]
+
+        def up_into_psum(u):
+            up_banks[u] = []
+            for b in range(2):
+                bank = psum_up.tile([P, 2, H_CHUNK], BF16, tag="up", name="up_bank")
+                for e in range(2):
+                    nc.tensor.matmul(out=bank[:, e, :], lhsT=identity_bf[:], rhs=up_sb[u][:, 2 * b + e, :], start=True, stop=True)
+                up_banks[u].append(bank)
+
+        def gate_factor(u):
+            factor = silu_tiles[u]
+            if u in up_banks:
+                for b in range(2):
+                    cols = slice(b * HALF_UNIT, (b + 1) * HALF_UNIT)
+                    nc.vector.scalar_tensor_tensor(
+                        out=factor[:, cols], in0=factor[:, cols], scalar=1.0,
+                        in1=up_banks[u][b][:].rearrange("p e h -> p (e h)"), op0=ALU.subtract, op1=ALU.mult,
+                    )
+            else:
+                nc.vector.scalar_tensor_tensor(
+                    out=factor[:], in0=factor[:], scalar=1.0, in1=up_sb[u][:].rearrange("p j h -> p (j h)"),
+                    op0=ALU.subtract, op1=ALU.mult,
+                )
+
+        def first_products(u):
+            hc, c = u // TOKEN_PASSES, u % TOKEN_PASSES
+            d_h_banks[u] = []
             for j in range(PACK):
-                d_h = psum_first.tile([P, H_CHUNK], FP32, tag="first")
+                d_h = psum_first.tile([P, H_CHUNK], FP32, tag="first", name="d_h")
                 nc.tensor.matmul_mx(
                     out=d_h[:],
                     lhsT=err_codes[:, c, j * P : (j + 1) * P].bitcast(FP8X4),
@@ -177,56 +254,152 @@ def tile_continuummemorysystem_pa_kernel(tc, err, W_down, gate_pre, up_pre, x_pr
                     start=True,
                     stop=True,
                 )
+                d_h_banks[u].append(d_h)
+
+        def halves(u):
+            half = tanh_tiles[u]
+            for j in range(PACK):
                 cols = slice(j * H_CHUNK, (j + 1) * H_CHUNK)
                 nc.vector.scalar_tensor_tensor(
-                    out=half[:, cols], in0=half[:, cols], scalar=1.0, in1=d_h[:], op0=ALU.add, op1=ALU.mult,
+                    out=half[:, cols], in0=half[:, cols], scalar=1.0, in1=d_h_banks[u][j][:], op0=ALU.add, op1=ALU.mult,
                 )
-            half_rows = half[:].rearrange("p (j h) -> p j h", j=PACK)
-            d_up = grouped_pool.tile([P, UNIT], BF16, tag="grouped", align_bytes=64)
-            nc.vector.tensor_tensor(out=by_word(d_up[:]), in0=by_column(half_rows), in1=by_column(gate_sb[hc, c][:]), op=ALU.mult)
-            d_gate = grouped_pool.tile([P, UNIT], BF16, tag="grouped", align_bytes=64)
-            factor_rows = gate_factor[:].rearrange("p (j h) -> p j h", j=PACK)
-            nc.vector.tensor_tensor(out=by_word(d_gate[:]), in0=by_column(half_rows), in1=by_column(factor_rows), op=ALU.mult)
-            quantise(d_up, up_words[:, c, :], up_planes[:, c, :])
-            quantise(d_gate, gate_words[:, c, :], gate_planes[:, c, :])
 
-        def second_products(hc, words, planes, column, out):
-            for m in range(M_TILES):
-                acc = psum_second.tile([P, FEATURES], FP32, tag="second")
+        def up_product(u):
+            pair_tiles[u] = pair_pool.tile([P, 2 * UNIT], BF16, tag="pair", align_bytes=64, name="pair")
+            half_rows = tanh_tiles[u][:].rearrange("p (j h) -> p j h", j=PACK)
+            nc.gpsimd.tensor_tensor(
+                out=by_word(pair_tiles[u][:, 0:UNIT]), in0=by_column(half_rows), in1=by_column(gate_sb[u][:]), op=ALU.mult,
+            )
+
+        def gate_product(u):
+            half_rows = tanh_tiles[u][:].rearrange("p (j h) -> p j h", j=PACK)
+            factor_rows = silu_tiles[u][:].rearrange("p (j h) -> p j h", j=PACK)
+            nc.vector.tensor_tensor(
+                out=by_word(pair_tiles[u][:, UNIT : 2 * UNIT]), in0=by_column(half_rows), in1=by_column(factor_rows), op=ALU.mult,
+            )
+
+        def quantise_product(u, which):
+            hc, c = u // TOKEN_PASSES, u % TOKEN_PASSES
+            if (hc, which) not in chunk_tiles:
+                words = chunk_codes.tile([P, TOKEN_PASSES, H_CHUNK], U32, align_bytes=64, tag="words_%d" % which, name="words")
+                planes = chunk_codes.tile([P, TOKEN_PASSES, H_CHUNK], U8, align_bytes=64, tag="planes_%d" % which, name="planes")
+                chunk_tiles[hc, which] = (words, planes)
+            words, planes = chunk_tiles[hc, which]
+            quantise(pair_tiles[u][:, which * UNIT : (which + 1) * UNIT], words[:, c, :], planes[:, c, :])
+
+        def second_pass(acc, hc, which, m, c):
+            words, planes = chunk_tiles[hc, which]
+            nc.tensor.matmul_mx(
+                out=acc[:],
+                lhsT=words[:, c, m * P : (m + 1) * P].bitcast(FP8X4),
+                lhsT_scale=planes[:, c, m * P : (m + 1) * P],
+                rhs=x_codes[:, c, :].bitcast(FP8X4),
+                rhs_scale=x_scales[:, c, :],
+                start=(c == 0),
+                stop=(c == TOKEN_PASSES - 1),
+            )
+
+        def leave(acc, hc, which, m, on_vector):
+            scaled = results.tile([P, FEATURES], FP32, tag="scaled", name="scaled")
+            if on_vector:
+                nc.vector.tensor_scalar_mul(out=scaled[:], in0=acc[:], scalar1=final_scale[:, which : which + 1])
+            else:
+                nc.scalar.activation(out=scaled[:], in_=acc[:], func=ACT.Copy, scale=final_scale[:, which : which + 1])
+            first_row = hc * H_CHUNK + m * P
+            nc.sync.dma_start(out=outs[which][first_row : first_row + P, :], in_=scaled[:])
+
+        for step in gate_function_pieces(0):
+            step[0](step[1], step[2])
+        transpose_err(0)
+        squares(0)
+        transpose_err(1)
+        squares(1)
+        regroup_err(0)
+        regroup_err(1)
+        regroup_rows("w0", w_sb[0])
+        for c in range(TOKEN_PASSES):
+            quantise(grouped_err[c][:], err_codes[:, c, :], err_scales[:, c, :])
+        gate_factor(0)
+        quantise(grouped_rows["w0"][:], w_codes[:, 0, :], w_scales[:, 0, :])
+        first_products(0)
+        diagonal_sums()
+        turned_sums = psum_second.tile([P, P], FP32, tag="second", name="turned_sums")
+        nc.tensor.transpose(turned_sums[:], repeated[:], identity[:])
+        for step in gate_function_pieces(1):
+            step[0](step[1], step[2])
+        up_into_psum(1)
+        halves(0)
+        up_product(0)
+        first_products(1)
+        regroup_rows("w1", w_sb[1])
+
+        open_groups = {}
+        for k in range(UNITS):
+            leaving = []
+            if k >= 2:
+                leaving = [((k - 2) // 2, (k - 2) % 2, m) for m in range(M_TILES)]
+            functions = gate_function_pieces(k + 2) if k + 2 < UNITS else []
+            if k >= 2 and k % 2 == 0 and k // 2 + 1 < H_CHUNKS:
+                regroup_rows("w%d" % (k // 2 + 1), w_sb[k // 2 + 1])
+            accs = {}
+            for tile_index in range(len(leaving[:2])):
+                hc, which, m = leaving[tile_index]
+                accs[tile_index] = psum_second.tile([P, FEATURES], FP32, tag="second", name="acc")
                 for c in range(TOKEN_PASSES):
-                    nc.tensor.matmul_mx(
-                        out=acc[:],
-                        lhsT=words[:, c, m * P : (m + 1) * P].bitcast(FP8X4),
-                        lhsT_scale=planes[:, c, m * P : (m + 1) * P],
-                        rhs=x_codes[:, c, :].bitcast(FP8X4),
-                        rhs_scale=x_scales[:, c, :],
-                        start=(c == 0),
-                        stop=(c == TOKEN_PASSES - 1),
-                    )
-                scaled = results.tile([P, FEATURES], FP32)
-                nc.scalar.activation(out=scaled[:], in_=acc[:], func=ACT.Copy, scale=final_scale[:, column : column + 1])
-                first_row = hc * H_CHUNK + m * P
-                nc.sync.dma_start(out=out[first_row : first_row + P, :], in_=scaled[:])
+                    second_pass(accs[tile_index], hc, which, m, c)
+            if k + 1 < UNITS:
+                gate_factor(k + 1)
+            if k + 2 < UNITS:
+                up_into_psum(k + 2)
+            if k + 1 < UNITS:
+                halves(k + 1)
+            for index in range(4):
+                if index < len(functions):
+                    step = functions[index]
+                    step[0](step[1], step[2])
+                if index == 2:
+                    for tile_index in range(2, len(leaving)):
+                        hc, which, m = leaving[tile_index]
+                        accs[tile_index] = psum_second.tile([P, FEATURES], FP32, tag="second", name="acc")
+                        for c in range(TOKEN_PASSES):
+                            second_pass(accs[tile_index], hc, which, m, c)
+                if index < len(leaving):
+                    hc, which, m = leaving[index]
+                    leave(accs[index], hc, which, m, False)
+            if k == 0:
+                regroup_rows("x0", x_sb[0])
+                regroup_rows("x1", x_sb[1])
+                total_of_squares(turned_sums)
+                nc.gpsimd.tensor_tensor(out=err_mag[:], in0=scaled_total[:], in1=one_half[:], op=ALU.pow)
+            if k == UNITS - 1:
+                for tile_index in range(6):
+                    which, m = tile_index // M_TILES, tile_index % M_TILES
+                    if tile_index < 4:
+                        open_groups[tile_index] = psum_first.tile([P, FEATURES], FP32, tag="first", name="acc_first")
+                    else:
+                        open_groups[tile_index] = psum_up.tile([P, FEATURES], FP32, tag="up", name="acc_up")
+                    second_pass(open_groups[tile_index], H_CHUNKS - 1, which, m, 0)
+            gate_product(k)
+            quantise_product(k, 0)
+            if k == 0:
+                surprise_gate()
+            if k == 1:
+                for c in range(TOKEN_PASSES):
+                    quantise(grouped_rows["x%d" % c][:], x_codes[:, c, :], x_scales[:, c, :])
+            if k % 2 == 0 and k // 2 + 1 < H_CHUNKS:
+                quantise(grouped_rows["w%d" % (k // 2 + 1)][:], w_codes[:, k // 2 + 1, :], w_scales[:, k // 2 + 1, :])
+            quantise_product(k, 1)
+            if k + 1 < UNITS:
+                up_product(k + 1)
+            if k + 2 < UNITS:
+                first_products(k + 2)
 
-        prepare_err(0)
-        prepare_rows(nc.vector.tensor_copy, w_sb[0], w_codes[:, 0, :], w_scales[:, 0, :])
-        gate_functions(0, 0)
-        prepare_err(1)
-        gate_functions(0, 1)
-        for hc in range(H_CHUNKS):
-            up_words = chunk_codes.tile([P, TOKEN_PASSES, H_CHUNK], U32, align_bytes=64)
-            up_planes = chunk_codes.tile([P, TOKEN_PASSES, H_CHUNK], U8, align_bytes=64)
-            gate_words = chunk_codes.tile([P, TOKEN_PASSES, H_CHUNK], U32, align_bytes=64)
-            gate_planes = chunk_codes.tile([P, TOKEN_PASSES, H_CHUNK], U8, align_bytes=64)
-            for c in range(TOKEN_PASSES):
-                pointwise(hc, c, up_words, up_planes, gate_words, gate_planes)
-                if hc + 1 < H_CHUNKS:
-                    gate_functions(hc + 1, c)
-                if hc == 0 and c == 0:
-                    surprise_gate()
-                    for cx in range(TOKEN_PASSES):
-                        prepare_rows(nc.scalar.copy, x_sb[cx], x_codes[:, cx, :], x_scales[:, cx, :])
-                if hc + 1 < H_CHUNKS and c == 0:
-                    prepare_rows(nc.scalar.copy, w_sb[hc + 1], w_codes[:, hc + 1, :], w_scales[:, hc + 1, :])
-            second_products(hc, up_words, up_planes, 0, out_0)
-            second_products(hc, gate_words, gate_planes, 1, out_1)
+        for tile_index in range(2 * M_TILES):
+            which, m = tile_index // M_TILES, tile_index % M_TILES
+            if tile_index in open_groups:
+                acc = open_groups[tile_index]
+            else:
+                acc = psum_second.tile([P, FEATURES], FP32, tag="second", name="acc")
+                second_pass(acc, H_CHUNKS - 1, which, m, 0)
+            second_pass(acc, H_CHUNKS - 1, which, m, 1)
+            leave(acc, H_CHUNKS - 1, which, m, tile_index % 2 == 1)

@@ -56,8 +56,12 @@ def tile_continuummemorysystem_pa_kernel(tc, err, W_down, gate_pre, up_pre, x_pr
 
         def load_err(c):
             err_sb[c] = inputs.tile([P, PACK * FEATURES], BF16, name="err_%d" % c)
-            rows = err[c * K_PASS : (c + 1) * K_PASS, :]
-            nc.sync.dma_start(out=err_sb[c][:], in_=rows.rearrange("(p j) d -> p (j d)", j=PACK))
+            rows = err[c * K_PASS : (c + 1) * K_PASS, :].rearrange("(p j) d -> p j d", j=PACK)
+            for pair in range(PACK // 2):
+                nc.sync.dma_start(
+                    out=err_sb[c][:, 2 * pair * FEATURES : 2 * (pair + 1) * FEATURES].rearrange("p (j d) -> p j d", j=2),
+                    in_=rows[:, 2 * pair : 2 * pair + 2, :],
+                )
 
         def load_x(c):
             x_sb[c] = inputs.tile([P, PACK, FEATURES], BF16, name="x_%d" % c)
@@ -84,9 +88,9 @@ def tile_continuummemorysystem_pa_kernel(tc, err, W_down, gate_pre, up_pre, x_pr
         def load_up(u):
             load_pre(up_sb, up_pre, "up", u)
 
-        load_gate(0)
         load_err(0)
         load_err(1)
+        load_gate(0)
         load_w(0)
         load_up(0)
         load_gate(1)
@@ -149,9 +153,9 @@ def tile_continuummemorysystem_pa_kernel(tc, err, W_down, gate_pre, up_pre, x_pr
                 )
             grouped_err[c] = grouped
 
-        def regroup_rows(key, rows):
+        def regroup_rows(copy, key, rows):
             grouped = grouped_pool.tile([P, UNIT], BF16, tag="grouped", align_bytes=64, name="grouped")
-            nc.scalar.copy(out=by_word(grouped[:]), in_=by_column(rows[:]))
+            copy(out=by_word(grouped[:]), in_=by_column(rows[:]))
             grouped_rows[key] = grouped
 
         final_scale = const.tile([P, 2], FP32)
@@ -308,17 +312,17 @@ def tile_continuummemorysystem_pa_kernel(tc, err, W_down, gate_pre, up_pre, x_pr
             first_row = hc * H_CHUNK + m * P
             nc.sync.dma_start(out=outs[which][first_row : first_row + P, :], in_=scaled[:])
 
-        for step in gate_function_pieces(0):
-            step[0](step[1], step[2])
         transpose_err(0)
-        squares(0)
         transpose_err(1)
+        squares(0)
         squares(1)
         regroup_err(0)
         regroup_err(1)
-        regroup_rows("w0", w_sb[0])
+        for step in gate_function_pieces(0):
+            step[0](step[1], step[2])
         for c in range(TOKEN_PASSES):
             quantise(grouped_err[c][:], err_codes[:, c, :], err_scales[:, c, :])
+        regroup_rows(nc.vector.tensor_copy, "w0", w_sb[0])
         gate_factor(0)
         quantise(grouped_rows["w0"][:], w_codes[:, 0, :], w_scales[:, 0, :])
         first_products(0)
@@ -331,54 +335,45 @@ def tile_continuummemorysystem_pa_kernel(tc, err, W_down, gate_pre, up_pre, x_pr
         halves(0)
         up_product(0)
         first_products(1)
-        regroup_rows("w1", w_sb[1])
+        regroup_rows(nc.scalar.copy, "w1", w_sb[1])
 
-        open_groups = {}
-        for k in range(UNITS):
+        for k in range(UNITS - 1):
             leaving = []
-            if k >= 2:
+            if 2 <= k < UNITS - 2:
                 leaving = [((k - 2) // 2, (k - 2) % 2, m) for m in range(M_TILES)]
+            if k == UNITS - 2:
+                leaving = [((k - 2) // 2, which, m) for which in range(2) for m in range(M_TILES)]
             functions = gate_function_pieces(k + 2) if k + 2 < UNITS else []
             if k >= 2 and k % 2 == 0 and k // 2 + 1 < H_CHUNKS:
-                regroup_rows("w%d" % (k // 2 + 1), w_sb[k // 2 + 1])
+                regroup_rows(nc.scalar.copy, "w%d" % (k // 2 + 1), w_sb[k // 2 + 1])
             accs = {}
-            for tile_index in range(len(leaving[:2])):
+
+            def both_passes(tile_index):
                 hc, which, m = leaving[tile_index]
                 accs[tile_index] = psum_second.tile([P, FEATURES], FP32, tag="second", name="acc")
                 for c in range(TOKEN_PASSES):
                     second_pass(accs[tile_index], hc, which, m, c)
-            if k + 1 < UNITS:
-                gate_factor(k + 1)
+
+            for tile_index in range(len(leaving[:2])):
+                both_passes(tile_index)
+            gate_factor(k + 1)
             if k + 2 < UNITS:
                 up_into_psum(k + 2)
-            if k + 1 < UNITS:
-                halves(k + 1)
-            for index in range(4):
+            halves(k + 1)
+            for index in range(max(len(functions), len(leaving))):
                 if index < len(functions):
                     step = functions[index]
                     step[0](step[1], step[2])
-                if index == 2:
-                    for tile_index in range(2, len(leaving)):
-                        hc, which, m = leaving[tile_index]
-                        accs[tile_index] = psum_second.tile([P, FEATURES], FP32, tag="second", name="acc")
-                        for c in range(TOKEN_PASSES):
-                            second_pass(accs[tile_index], hc, which, m, c)
                 if index < len(leaving):
                     hc, which, m = leaving[index]
                     leave(accs[index], hc, which, m, False)
+                if index + 2 < len(leaving):
+                    both_passes(index + 2)
             if k == 0:
-                regroup_rows("x0", x_sb[0])
-                regroup_rows("x1", x_sb[1])
+                regroup_rows(nc.scalar.copy, "x0", x_sb[0])
+                regroup_rows(nc.scalar.copy, "x1", x_sb[1])
                 total_of_squares(turned_sums)
                 nc.gpsimd.tensor_tensor(out=err_mag[:], in0=scaled_total[:], in1=one_half[:], op=ALU.pow)
-            if k == UNITS - 1:
-                for tile_index in range(6):
-                    which, m = tile_index // M_TILES, tile_index % M_TILES
-                    if tile_index < 4:
-                        open_groups[tile_index] = psum_first.tile([P, FEATURES], FP32, tag="first", name="acc_first")
-                    else:
-                        open_groups[tile_index] = psum_up.tile([P, FEATURES], FP32, tag="up", name="acc_up")
-                    second_pass(open_groups[tile_index], H_CHUNKS - 1, which, m, 0)
             gate_product(k)
             quantise_product(k, 0)
             if k == 0:
@@ -389,17 +384,48 @@ def tile_continuummemorysystem_pa_kernel(tc, err, W_down, gate_pre, up_pre, x_pr
             if k % 2 == 0 and k // 2 + 1 < H_CHUNKS:
                 quantise(grouped_rows["w%d" % (k // 2 + 1)][:], w_codes[:, k // 2 + 1, :], w_scales[:, k // 2 + 1, :])
             quantise_product(k, 1)
-            if k + 1 < UNITS:
+            if k + 1 < UNITS - 1:
                 up_product(k + 1)
             if k + 2 < UNITS:
                 first_products(k + 2)
 
-        for tile_index in range(2 * M_TILES):
-            which, m = tile_index // M_TILES, tile_index % M_TILES
-            if tile_index in open_groups:
-                acc = open_groups[tile_index]
-            else:
-                acc = psum_second.tile([P, FEATURES], FP32, tag="second", name="acc")
-                second_pass(acc, H_CHUNKS - 1, which, m, 0)
-            second_pass(acc, H_CHUNKS - 1, which, m, 1)
-            leave(acc, H_CHUNKS - 1, which, m, tile_index % 2 == 1)
+        last = UNITS - 1
+        last_chunk = H_CHUNKS - 1
+        open_groups = {}
+        for m in range(M_TILES):
+            for which in range(2):
+                if m < 2:
+                    open_groups[which, m] = psum_first.tile([P, FEATURES], FP32, tag="first", name="acc_first")
+                elif m == 2:
+                    open_groups[which, m] = psum_up.tile([P, FEATURES], FP32, tag="up", name="acc_up")
+                else:
+                    open_groups[which, m] = psum_second.tile([P, FEATURES], FP32, tag="second", name="acc")
+                second_pass(open_groups[which, m], last_chunk, which, m, 0)
+        pair_tiles[last] = pair_pool.tile([P, 2 * UNIT], BF16, tag="pair", align_bytes=64, name="pair")
+        half_rows = tanh_tiles[last][:].rearrange("p (j h) -> p j h", j=PACK)
+        factor_rows = silu_tiles[last][:].rearrange("p (j h) -> p j h", j=PACK)
+        other_rows = (gate_sb[last][:], factor_rows)
+
+        def finish_piece(m, last_on_vector):
+            for which in range(2):
+                words, planes = chunk_tiles[last_chunk, which]
+                first = which * UNIT + m * PACK * P
+                quantise(
+                    pair_tiles[last][:, first : first + PACK * P],
+                    words[:, 1, m * P : (m + 1) * P], planes[:, 1, m * P : (m + 1) * P],
+                )
+            for which in range(2):
+                second_pass(open_groups[which, m], last_chunk, which, m, 1)
+                leave(open_groups[which, m], last_chunk, which, m, last_on_vector and which == 1)
+
+        for m in range(M_TILES):
+            cols = slice(m * P, (m + 1) * P)
+            for which in range(2):
+                first = which * UNIT + m * PACK * P
+                nc.vector.tensor_tensor(
+                    out=by_word(pair_tiles[last][:, first : first + PACK * P]), in0=by_column(half_rows[:, :, cols]),
+                    in1=by_column(other_rows[which][:, :, cols]), op=ALU.mult,
+                )
+            if m >= 1:
+                finish_piece(m - 1, False)
+        finish_piece(M_TILES - 1, True)

@@ -22,7 +22,7 @@ M_TILES = H_CHUNK // P
 UNIT = PACK * H_CHUNK
 UNITS = H_CHUNKS * TOKEN_PASSES
 HALF_UNIT = UNIT // 2
-RUN = 4
+RUN = 8
 
 FLOPS = 3 * 2 * TOKENS * FEATURES * HIDDEN
 

from contextlib import ExitStack

import concourse.mybir as mybir
from concourse.masks import make_identity

FP32 = mybir.dt.float32
BF16 = mybir.dt.bfloat16
U32 = mybir.dt.uint32
U8 = mybir.dt.uint8
FP8X4 = mybir.dt.float8_e4m3fn_x4
ACT = mybir.ActivationFunctionType
ALU = mybir.AluOpType

P = 128
PACK = 4
K_PASS = P * PACK
TOKENS, FEATURES, HIDDEN = 1024, 512, 2048
TOKEN_PASSES = TOKENS // K_PASS
H_CHUNK = 512
H_CHUNKS = HIDDEN // H_CHUNK
M_TILES = H_CHUNK // P
UNIT = PACK * H_CHUNK
UNITS = H_CHUNKS * TOKEN_PASSES
HALF_UNIT = UNIT // 2
RUN = 8

FLOPS = 3 * 2 * TOKENS * FEATURES * HIDDEN


def by_column(rows):
    return rows.rearrange("p t (c i) -> p c t i", i=RUN)


def by_word(grouped):
    return grouped.rearrange("p (c i t) -> p c t i", i=RUN, t=PACK)


def tile_continuummemorysystem_pa_kernel(tc, err, W_down, gate_pre, up_pre, x_pred, out_0, out_1):
    nc = tc.nc
    outs = (out_0, out_1)
    with ExitStack() as pools:
        const = pools.enter_context(tc.tile_pool(name="const", bufs=1))
        inputs = pools.enter_context(tc.tile_pool(name="inputs", bufs=1))
        codes = pools.enter_context(tc.tile_pool(name="codes", bufs=1))
        chunk_codes = pools.enter_context(tc.tile_pool(name="chunk_codes", bufs=2))
        grouped_pool = pools.enter_context(tc.tile_pool(name="grouped", bufs=3))
        pair_pool = pools.enter_context(tc.tile_pool(name="pair", bufs=1))
        work = pools.enter_context(tc.tile_pool(name="work", bufs=3))
        results = pools.enter_context(tc.tile_pool(name="results", bufs=6))
        psum_first = pools.enter_context(tc.psum_pool(name="psum_first", bufs=4))
        psum_up = pools.enter_context(tc.psum_pool(name="psum_up", bufs=2))
        psum_second = pools.enter_context(tc.psum_pool(name="psum_second", bufs=2))
        pools.enter_context(tc.manual_schedule())

        err_sb, x_sb, w_sb, gate_sb, up_sb = {}, {}, {}, {}, {}

        def load_err(c):
            err_sb[c] = inputs.tile([P, PACK * FEATURES], BF16, name="err_%d" % c)
            rows = err[c * K_PASS : (c + 1) * K_PASS, :].rearrange("(p j) d -> p j d", j=PACK)
            for pair in range(PACK // 2):
                nc.sync.dma_start(
                    out=err_sb[c][:, 2 * pair * FEATURES : 2 * (pair + 1) * FEATURES].rearrange("p (j d) -> p j d", j=2),
                    in_=rows[:, 2 * pair : 2 * pair + 2, :],
                )

        def load_x(c):
            x_sb[c] = inputs.tile([P, PACK, FEATURES], BF16, name="x_%d" % c)
            rows = x_pred[c * K_PASS : (c + 1) * K_PASS, :]
            nc.sync.dma_start(out=x_sb[c][:], in_=rows.rearrange("(p j) d -> p j d", j=PACK))

        def load_w(hc):
            w_sb[hc] = inputs.tile([P, PACK, H_CHUNK], BF16, name="w_%d" % hc)
            cols = slice(hc * H_CHUNK, (hc + 1) * H_CHUNK)
            for u in range(2):
                rows = W_down[u * 2 * P : (u + 1) * 2 * P, cols]
                nc.sync.dma_start(out=w_sb[hc][:, 2 * u : 2 * u + 2, :], in_=rows.rearrange("(q e) n -> q e n", e=2))

        def load_pre(kept, source, label, u):
            hc, c = u // TOKEN_PASSES, u % TOKEN_PASSES
            cols = slice(hc * H_CHUNK, (hc + 1) * H_CHUNK)
            toks = slice(c * K_PASS, (c + 1) * K_PASS)
            kept[u] = inputs.tile([P, PACK, H_CHUNK], BF16, name="%s_%d" % (label, u))
            nc.sync.dma_start(out=kept[u][:], in_=source[toks, cols].rearrange("(p j) h -> p j h", j=PACK))

        def load_gate(u):
            load_pre(gate_sb, gate_pre, "gate", u)

        def load_up(u):
            load_pre(up_sb, up_pre, "up", u)

        load_err(0)
        load_err(1)
        load_gate(0)
        load_w(0)
        load_up(0)
        load_gate(1)
        load_up(1)
        load_w(1)
        load_gate(2)
        load_up(2)
        load_x(0)
        load_x(1)
        load_gate(3)
        load_up(3)
        for hc in range(2, H_CHUNKS):
            load_w(hc)
            for u in (2 * hc, 2 * hc + 1):
                load_gate(u)
                load_up(u)

        warm = const.tile([P, 1], FP32)
        nc.gpsimd.memset(warm[:], 0.0)
        identity = const.tile([P, P], FP32)
        make_identity(nc, identity[:])
        identity_bf = const.tile([P, P], BF16)
        make_identity(nc, identity_bf[:])
        one_half = const.tile([P, 1], FP32)
        nc.gpsimd.memset(one_half[:], 0.5)
        warmed = const.tile([P, 1], FP32)
        nc.scalar.activation(out=warmed[:], in_=warm[:], func=ACT.Tanh)

        err_codes = codes.tile([P, TOKEN_PASSES, K_PASS], U32, align_bytes=64)
        err_scales = codes.tile([P, TOKEN_PASSES, K_PASS], U8, align_bytes=64)
        x_codes = codes.tile([P, TOKEN_PASSES, FEATURES], U32, align_bytes=64)
        x_scales = codes.tile([P, TOKEN_PASSES, FEATURES], U8, align_bytes=64)
        w_codes = codes.tile([P, H_CHUNKS, H_CHUNK], U32, align_bytes=64)
        w_scales = codes.tile([P, H_CHUNKS, H_CHUNK], U8, align_bytes=64)

        def quantise(grouped, words, scales):
            nc.vector.quantize_mx(out=words.bitcast(FP8X4), scales=scales, in_=grouped)

        turned_err, grouped_err, grouped_rows = {}, {}, {}

        def transpose_err(c):
            err_words = err_sb[c][:].bitcast(FP32)
            turned_err[c] = []
            for pair in range(PACK // 2):
                turned = psum_first.tile([P, 2, 2, P], FP32, tag="first", name="turned")
                for b in range(2):
                    j = 2 * pair + b
                    for u in range(2):
                        first_word = (2 * j + u) * P
                        nc.tensor.transpose(turned[:, b, u, :], err_words[:, first_word : first_word + P], identity[:])
                turned_err[c].append(turned)

        def regroup_err(c):
            grouped = grouped_pool.tile([P, UNIT], BF16, tag="grouped", align_bytes=64, name="grouped")
            grouped_words = grouped[:].bitcast(FP32).rearrange("q (j p u) -> q j p u", j=PACK, u=2)
            for pair in range(PACK // 2):
                nc.vector.tensor_copy(
                    out=grouped_words[:, 2 * pair : 2 * pair + 2, :, :],
                    in_=turned_err[c][pair][:].rearrange("q b u p -> q b p u"),
                )
            grouped_err[c] = grouped

        def regroup_rows(copy, key, rows):
            grouped = grouped_pool.tile([P, UNIT], BF16, tag="grouped", align_bytes=64, name="grouped")
            copy(out=by_word(grouped[:]), in_=by_column(rows[:]))
            grouped_rows[key] = grouped

        final_scale = const.tile([P, 2], FP32)
        square_bank = psum_second.tile([P, P], FP32, tag="second", name="square_bank")
        repeated = const.tile([P, P], FP32)
        scaled_total = const.tile([P, 1], FP32)
        err_mag = const.tile([P, 1], FP32)

        def squares(c):
            for j in range(PACK):
                for b in range(FEATURES // P):
                    block = err_sb[c][:, j * FEATURES + b * P : j * FEATURES + (b + 1) * P]
                    nc.tensor.matmul(
                        out=square_bank[:], lhsT=block, rhs=block,
                        start=(c == 0 and j == 0 and b == 0),
                        stop=(c == TOKEN_PASSES - 1 and j == PACK - 1 and b == FEATURES // P - 1),
                    )

        def diagonal_sums():
            masked = const.tile([P, P], FP32)
            row_sum = const.tile([P, 1], FP32)
            nc.vector.scalar_tensor_tensor(
                out=masked[:], in0=square_bank[:], scalar=1.0, in1=identity[:], op0=ALU.mult, op1=ALU.mult,
                accum_out=row_sum[:],
            )
            nc.vector.tensor_copy(out=repeated[:], in_=row_sum[:, 0:1].to_broadcast([P, P]))

        def total_of_squares(turned):
            total = const.tile([P, 1], FP32)
            nc.vector.reduce_sum(out=total[:], in_=turned[:], axis=mybir.AxisListType.X)
            nc.vector.tensor_scalar_mul(out=scaled_total[:], in0=total[:], scalar1=1.0 / (TOKENS * TOKENS))

        def surprise_gate():
            ema = const.tile([P, 1], FP32)
            nc.vector.tensor_scalar(out=ema[:], in0=err_mag[:], scalar1=0.05, scalar2=0.95, op0=ALU.mult, op1=ALU.add)
            nc.vector.tensor_scalar_max(out=ema[:], in0=ema[:], scalar1=1e-8)
            inverse = const.tile([P, 1], FP32)
            nc.vector.reciprocal(out=inverse[:], in_=ema[:])
            ratio = const.tile([P, 1], FP32)
            nc.vector.tensor_mul(out=ratio[:], in0=err_mag[:], in1=inverse[:])
            for column, factor in ((0, 2.0), (1, -2.0)):
                nc.vector.tensor_scalar(
                    out=final_scale[:, column : column + 1], in0=ratio[:],
                    scalar1=3.0, scalar2=1.0 / (factor * TOKENS), op0=ALU.min, op1=ALU.mult,
                )

        tanh_tiles, silu_tiles, d_h_banks, up_banks, pair_tiles, chunk_tiles = {}, {}, {}, {}, {}, {}

        def silu_piece(u, piece):
            if piece == 0:
                silu_tiles[u] = work.tile([P, UNIT], FP32, tag="silu", name="silu_neg")
            cols = slice(piece * HALF_UNIT, (piece + 1) * HALF_UNIT)
            gate_flat = gate_sb[u][:].rearrange("p j h -> p (j h)")
            nc.scalar.activation(out=silu_tiles[u][:, cols], in_=gate_flat[:, cols], func=ACT.Silu, scale=-1.0)

        def tanh_piece(u, piece):
            if piece == 0:
                tanh_tiles[u] = work.tile([P, UNIT], FP32, tag="tanh", name="tanh_half")
            cols = slice(piece * HALF_UNIT, (piece + 1) * HALF_UNIT)
            gate_flat = gate_sb[u][:].rearrange("p j h -> p (j h)")
            nc.scalar.activation(out=tanh_tiles[u][:, cols], in_=gate_flat[:, cols], func=ACT.Tanh, scale=0.5)

        def gate_function_pieces(u):
            return [(silu_piece, u, 0), (silu_piece, u, 1), (tanh_piece, u, 0), (tanh_piece, u, 1)]

        def up_into_psum(u):
            up_banks[u] = []
            for b in range(2):
                bank = psum_up.tile([P, 2, H_CHUNK], BF16, tag="up", name="up_bank")
                for e in range(2):
                    nc.tensor.matmul(out=bank[:, e, :], lhsT=identity_bf[:], rhs=up_sb[u][:, 2 * b + e, :], start=True, stop=True)
                up_banks[u].append(bank)

        def gate_factor(u):
            factor = silu_tiles[u]
            if u in up_banks:
                for b in range(2):
                    cols = slice(b * HALF_UNIT, (b + 1) * HALF_UNIT)
                    nc.vector.scalar_tensor_tensor(
                        out=factor[:, cols], in0=factor[:, cols], scalar=1.0,
                        in1=up_banks[u][b][:].rearrange("p e h -> p (e h)"), op0=ALU.subtract, op1=ALU.mult,
                    )
            else:
                nc.vector.scalar_tensor_tensor(
                    out=factor[:], in0=factor[:], scalar=1.0, in1=up_sb[u][:].rearrange("p j h -> p (j h)"),
                    op0=ALU.subtract, op1=ALU.mult,
                )

        def first_products(u):
            hc, c = u // TOKEN_PASSES, u % TOKEN_PASSES
            d_h_banks[u] = []
            for j in range(PACK):
                d_h = psum_first.tile([P, H_CHUNK], FP32, tag="first", name="d_h")
                nc.tensor.matmul_mx(
                    out=d_h[:],
                    lhsT=err_codes[:, c, j * P : (j + 1) * P].bitcast(FP8X4),
                    lhsT_scale=err_scales[:, c, j * P : (j + 1) * P],
                    rhs=w_codes[:, hc, :].bitcast(FP8X4),
                    rhs_scale=w_scales[:, hc, :],
                    start=True,
                    stop=True,
                )
                d_h_banks[u].append(d_h)

        def halves(u):
            half = tanh_tiles[u]
            for j in range(PACK):
                cols = slice(j * H_CHUNK, (j + 1) * H_CHUNK)
                nc.vector.scalar_tensor_tensor(
                    out=half[:, cols], in0=half[:, cols], scalar=1.0, in1=d_h_banks[u][j][:], op0=ALU.add, op1=ALU.mult,
                )

        def up_product(u):
            pair_tiles[u] = pair_pool.tile([P, 2 * UNIT], BF16, tag="pair", align_bytes=64, name="pair")
            half_rows = tanh_tiles[u][:].rearrange("p (j h) -> p j h", j=PACK)
            nc.gpsimd.tensor_tensor(
                out=by_word(pair_tiles[u][:, 0:UNIT]), in0=by_column(half_rows), in1=by_column(gate_sb[u][:]), op=ALU.mult,
            )

        def gate_product(u):
            half_rows = tanh_tiles[u][:].rearrange("p (j h) -> p j h", j=PACK)
            factor_rows = silu_tiles[u][:].rearrange("p (j h) -> p j h", j=PACK)
            nc.vector.tensor_tensor(
                out=by_word(pair_tiles[u][:, UNIT : 2 * UNIT]), in0=by_column(half_rows), in1=by_column(factor_rows), op=ALU.mult,
            )

        def quantise_product(u, which):
            hc, c = u // TOKEN_PASSES, u % TOKEN_PASSES
            if (hc, which) not in chunk_tiles:
                words = chunk_codes.tile([P, TOKEN_PASSES, H_CHUNK], U32, align_bytes=64, tag="words_%d" % which, name="words")
                planes = chunk_codes.tile([P, TOKEN_PASSES, H_CHUNK], U8, align_bytes=64, tag="planes_%d" % which, name="planes")
                chunk_tiles[hc, which] = (words, planes)
            words, planes = chunk_tiles[hc, which]
            quantise(pair_tiles[u][:, which * UNIT : (which + 1) * UNIT], words[:, c, :], planes[:, c, :])

        def second_pass(acc, hc, which, m, c):
            words, planes = chunk_tiles[hc, which]
            nc.tensor.matmul_mx(
                out=acc[:],
                lhsT=words[:, c, m * P : (m + 1) * P].bitcast(FP8X4),
                lhsT_scale=planes[:, c, m * P : (m + 1) * P],
                rhs=x_codes[:, c, :].bitcast(FP8X4),
                rhs_scale=x_scales[:, c, :],
                start=(c == 0),
                stop=(c == TOKEN_PASSES - 1),
            )

        def leave(acc, hc, which, m, on_vector):
            scaled = results.tile([P, FEATURES], FP32, tag="scaled", name="scaled")
            if on_vector:
                nc.vector.tensor_scalar_mul(out=scaled[:], in0=acc[:], scalar1=final_scale[:, which : which + 1])
            else:
                nc.scalar.activation(out=scaled[:], in_=acc[:], func=ACT.Copy, scale=final_scale[:, which : which + 1])
            first_row = hc * H_CHUNK + m * P
            nc.sync.dma_start(out=outs[which][first_row : first_row + P, :], in_=scaled[:])

        transpose_err(0)
        transpose_err(1)
        squares(0)
        squares(1)
        regroup_err(0)
        regroup_err(1)
        for step in gate_function_pieces(0):
            step[0](step[1], step[2])
        for c in range(TOKEN_PASSES):
            quantise(grouped_err[c][:], err_codes[:, c, :], err_scales[:, c, :])
        regroup_rows(nc.vector.tensor_copy, "w0", w_sb[0])
        gate_factor(0)
        quantise(grouped_rows["w0"][:], w_codes[:, 0, :], w_scales[:, 0, :])
        first_products(0)
        diagonal_sums()
        turned_sums = psum_second.tile([P, P], FP32, tag="second", name="turned_sums")
        nc.tensor.transpose(turned_sums[:], repeated[:], identity[:])
        for step in gate_function_pieces(1):
            step[0](step[1], step[2])
        up_into_psum(1)
        halves(0)
        up_product(0)
        first_products(1)
        regroup_rows(nc.scalar.copy, "w1", w_sb[1])

        for k in range(UNITS - 1):
            leaving = []
            if 2 <= k < UNITS - 2:
                leaving = [((k - 2) // 2, (k - 2) % 2, m) for m in range(M_TILES)]
            if k == UNITS - 2:
                leaving = [((k - 2) // 2, which, m) for which in range(2) for m in range(M_TILES)]
            functions = gate_function_pieces(k + 2) if k + 2 < UNITS else []
            if k >= 2 and k % 2 == 0 and k // 2 + 1 < H_CHUNKS:
                regroup_rows(nc.scalar.copy, "w%d" % (k // 2 + 1), w_sb[k // 2 + 1])
            accs = {}

            def both_passes(tile_index):
                hc, which, m = leaving[tile_index]
                accs[tile_index] = psum_second.tile([P, FEATURES], FP32, tag="second", name="acc")
                for c in range(TOKEN_PASSES):
                    second_pass(accs[tile_index], hc, which, m, c)

            for tile_index in range(len(leaving[:2])):
                both_passes(tile_index)
            gate_factor(k + 1)
            if k + 2 < UNITS:
                up_into_psum(k + 2)
            halves(k + 1)
            for index in range(max(len(functions), len(leaving))):
                if index < len(functions):
                    step = functions[index]
                    step[0](step[1], step[2])
                if index < len(leaving):
                    hc, which, m = leaving[index]
                    leave(accs[index], hc, which, m, False)
                if index + 2 < len(leaving):
                    both_passes(index + 2)
            if k == 0:
                regroup_rows(nc.scalar.copy, "x0", x_sb[0])
                regroup_rows(nc.scalar.copy, "x1", x_sb[1])
                total_of_squares(turned_sums)
                nc.gpsimd.tensor_tensor(out=err_mag[:], in0=scaled_total[:], in1=one_half[:], op=ALU.pow)
            gate_product(k)
            quantise_product(k, 0)
            if k == 0:
                surprise_gate()
            if k == 1:
                for c in range(TOKEN_PASSES):
                    quantise(grouped_rows["x%d" % c][:], x_codes[:, c, :], x_scales[:, c, :])
            if k % 2 == 0 and k // 2 + 1 < H_CHUNKS:
                quantise(grouped_rows["w%d" % (k // 2 + 1)][:], w_codes[:, k // 2 + 1, :], w_scales[:, k // 2 + 1, :])
            quantise_product(k, 1)
            if k + 1 < UNITS - 1:
                up_product(k + 1)
            if k + 2 < UNITS:
                first_products(k + 2)

        last = UNITS - 1
        last_chunk = H_CHUNKS - 1
        open_groups = {}
        for m in range(M_TILES):
            for which in range(2):
                if m < 2:
                    open_groups[which, m] = psum_first.tile([P, FEATURES], FP32, tag="first", name="acc_first")
                elif m == 2:
                    open_groups[which, m] = psum_up.tile([P, FEATURES], FP32, tag="up", name="acc_up")
                else:
                    open_groups[which, m] = psum_second.tile([P, FEATURES], FP32, tag="second", name="acc")
                second_pass(open_groups[which, m], last_chunk, which, m, 0)
        pair_tiles[last] = pair_pool.tile([P, 2 * UNIT], BF16, tag="pair", align_bytes=64, name="pair")
        half_rows = tanh_tiles[last][:].rearrange("p (j h) -> p j h", j=PACK)
        factor_rows = silu_tiles[last][:].rearrange("p (j h) -> p j h", j=PACK)
        other_rows = (gate_sb[last][:], factor_rows)

        def finish_piece(m, last_on_vector):
            for which in range(2):
                words, planes = chunk_tiles[last_chunk, which]
                first = which * UNIT + m * PACK * P
                quantise(
                    pair_tiles[last][:, first : first + PACK * P],
                    words[:, 1, m * P : (m + 1) * P], planes[:, 1, m * P : (m + 1) * P],
                )
            for which in range(2):
                second_pass(open_groups[which, m], last_chunk, which, m, 1)
                leave(open_groups[which, m], last_chunk, which, m, last_on_vector and which == 1)

        for m in range(M_TILES):
            cols = slice(m * P, (m + 1) * P)
            for which in range(2):
                first = which * UNIT + m * PACK * P
                nc.vector.tensor_tensor(
                    out=by_word(pair_tiles[last][:, first : first + PACK * P]), in0=by_column(half_rows[:, :, cols]),
                    in1=by_column(other_rows[which][:, :, cols]), op=ALU.mult,
                )
            if m >= 1:
                finish_piece(m - 1, False)
        finish_piece(M_TILES - 1, True)
